import numpy as np
import ml_dtypes

BF16 = ml_dtypes.bfloat16


def bf(x):
    return np.asarray(x, np.float32).astype(BF16)


def f32(x):
    return np.asarray(x, np.float32)


def f64(x):
    return np.asarray(x).astype(np.float64)


def striped(idx):
    return np.tile(idx.reshape(-1, 16).T, (8, 1))


S, D, M, Q, N = 1024, 128, 256, 256, 512


def setup_inputs():
    return {"table": bf(np.random.standard_normal((S, D))), "w1": bf(np.random.standard_normal((D, M)) / np.sqrt(D)), "b1": f32(0.1 * np.random.standard_normal((M, 1))), "w2": bf(np.random.standard_normal((M, Q)) / np.sqrt(M)), "b2": f32(0.1 * np.random.standard_normal((Q, 1))), "offs": striped(np.random.permutation(S)[:N])}


def reference(table, w1, b1, w2, b2, offs):
    idx = offs[:16].T.reshape(-1)
    h = np.maximum(f64(w1).T @ f64(table)[idx].T + f64(b1), 0.0)
    y = f64(w2).T @ h + f64(b2)
    return y / np.sqrt(np.sum(y * y, axis=0, keepdims=True))

@@ -1,0 +1,106 @@
+import concourse.mybir as mybir
+from concourse.masks import make_identity
+
+S, D, M, Q, N = 1024, 128, 256, 256, 512
+P = 128
+
+BF16, F32, U16 = mybir.dt.bfloat16, mybir.dt.float32, mybir.dt.uint16
+ACT = mybir.ActivationFunctionType
+ALU = mybir.AluOpType
+
+FLOPS = 2 * N * (D * M + M * Q)
+BYTES = 2 * N * D + 2 * D * M + 4 * M + 2 * M * Q + 4 * Q + 2 * P * (N // 16) + 4 * Q * N
+
+
+def tile_npmlphead_kernel(tc, table, w1, b1, w2, b2, offs, out):
+    nc = tc.nc
+    row_blocks = S // P
+    half_blocks = row_blocks // 2
+    with (
+        tc.tile_pool(name="held", bufs=1) as held,
+        tc.psum_pool(name="psum", bufs=1) as psum,
+    ):
+        offsets = held.tile([P, N // 16], U16, name="offsets")
+        nc.sync.dma_start(offsets[:], offs)
+
+        blocked = table.rearrange("(b p) d -> p b d", p=P)
+        rows = [held.tile([P, half_blocks, D], BF16, name=f"rows{h}") for h in range(2)]
+        nc.sync.dma_start(rows[0][:], blocked[:, 0:half_blocks, :])
+        nc.scalar.dma_start(rows[1][:], blocked[:, half_blocks:row_blocks, :])
+
+        identity = held.tile([P, P], BF16, name="identity")
+        make_identity(nc, identity[:])
+        ones = held.tile([P, P], F32, name="ones")
+        nc.vector.memset(ones[:], 1.0)
+
+        w1_sb = held.tile([D, M], BF16, name="w1_sb")
+        nc.scalar.dma_start(w1_sb[:], w1)
+        w2_sb = held.tile([P, M // P, Q], BF16, name="w2_sb")
+        nc.gpsimd.dma_start(w2_sb[:], w2.rearrange("(b p) q -> p b q", p=P))
+        b1_sb = held.tile([P, M // P], F32, name="b1_sb")
+        b2_sb = held.tile([P, Q // P], F32, name="b2_sb")
+        with nc.allow_non_contiguous_dma(reason="256 floats, one to a partition"):
+            nc.gpsimd.dma_start(b1_sb[:], b1.rearrange("(b p) o -> p (b o)", p=P))
+            nc.gpsimd.dma_start(b2_sb[:], b2.rearrange("(b p) o -> p (b o)", p=P))
+
+        window = held.tile([D, S], BF16, name="window")
+        for h in range(2):
+            flipped = psum.tile([D, half_blocks * P], BF16, name=f"flipped{h}")
+            for k in range(half_blocks):
+                nc.tensor.transpose(flipped[:, k * P : (k + 1) * P], rows[h][:, k, :], identity[:])
+            half = window[:, h * half_blocks * P : (h + 1) * half_blocks * P]
+            if h == 0:
+                nc.vector.tensor_copy(half, flipped[:])
+            else:
+                nc.scalar.copy(half, flipped[:])
+
+        hidden = []
+        for mb in range(M // P):
+            hidden_ps = psum.tile([P, N], F32, name=f"hidden_ps{mb}")
+            nc.tensor.matmul(
+                hidden_ps[:],
+                w1_sb[:, mb * P : (mb + 1) * P],
+                window[:].indirect(offsets[:]),
+                start=True,
+                stop=True,
+            )
+            hidden_mb = held.tile([P, N], BF16, name=f"hidden{mb}")
+            if mb == 0:
+                nc.scalar.activation(hidden_mb[:], hidden_ps[:], ACT.Relu, bias=b1_sb[:, mb : mb + 1])
+            else:
+                nc.vector.tensor_scalar(
+                    hidden_mb[:], hidden_ps[:], b1_sb[:, mb : mb + 1], 0.0, op0=ALU.add, op1=ALU.max
+                )
+            hidden.append(hidden_mb)
+
+        y_ps = []
+        squares = []
+        for qb in range(Q // P):
+            y_qb = psum.tile([P, N], F32, name=f"y_ps{qb}")
+            for mb in range(M // P):
+                nc.tensor.matmul(
+                    y_qb[:],
+                    w2_sb[:, mb, qb * P : (qb + 1) * P],
+                    hidden[mb][:],
+                    start=(mb == 0),
+                    stop=(mb == M // P - 1),
+                )
+            square_qb = held.tile([P, N], F32, name=f"square{qb}")
+            nc.scalar.activation(square_qb[:], y_qb[:], ACT.Square, bias=b2_sb[:, qb : qb + 1])
+            y_ps.append(y_qb)
+            squares.append(square_qb)
+
+        sumsq_ps = psum.tile([P, N], F32, name="sumsq_ps")
+        for qb in range(Q // P):
+            nc.tensor.matmul(
+                sumsq_ps[:], ones[:], squares[qb][:], start=(qb == 0), stop=(qb == Q // P - 1)
+            )
+        inv_norm = held.tile([P, N], F32, name="inv_norm")
+        nc.scalar.activation(inv_norm[:], sumsq_ps[:], ACT.Abs_reciprocal_sqrt)
+
+        for qb in range(Q // P):
+            result = held.tile([P, N], F32, name=f"result{qb}")
+            nc.vector.scalar_tensor_tensor(
+                result[:], y_ps[qb][:], b2_sb[:, qb : qb + 1], inv_norm[:], op0=ALU.add, op1=ALU.mult
+            )
+            nc.sync.dma_start(out[qb * P : (qb + 1) * P, :], result[:])

@@ -20,28 +20,29 @@ def tile_npmlphead_kernel(tc, table, w1, b1, w2, b2, offs, out):
         tc.tile_pool(name="held", bufs=1) as held,
         tc.psum_pool(name="psum", bufs=1) as psum,
     ):
-        offsets = held.tile([P, N // 16], U16, name="offsets")
-        nc.sync.dma_start(offsets[:], offs)
-
         blocked = table.rearrange("(b p) d -> p b d", p=P)
         rows = [held.tile([P, half_blocks, D], BF16, name=f"rows{h}") for h in range(2)]
         nc.sync.dma_start(rows[0][:], blocked[:, 0:half_blocks, :])
         nc.scalar.dma_start(rows[1][:], blocked[:, half_blocks:row_blocks, :])
 
+        offsets = held.tile([P, N // 16], U16, name="offsets")
+        nc.sync.dma_start(offsets[:], offs)
+        w1_sb = held.tile([D, M], BF16, name="w1_sb")
+        nc.scalar.dma_start(w1_sb[:], w1)
+        b1_sb = held.tile([P, M // P], F32, name="b1_sb")
+        b2_sb = held.tile([P, Q // P], F32, name="b2_sb")
+        with nc.allow_non_contiguous_dma(reason="256 floats, one to a partition"):
+            nc.sync.dma_start(b1_sb[:], b1.rearrange("(b p) o -> p (b o)", p=P))
+            nc.sync.dma_start(b2_sb[:], b2.rearrange("(b p) o -> p (b o)", p=P))
+        w2_sb = held.tile([P, M // P, Q], BF16, name="w2_sb")
+        nc.scalar.dma_start(w2_sb[:], w2.rearrange("(b p) q -> p b q", p=P))
+
         identity = held.tile([P, P], BF16, name="identity")
         make_identity(nc, identity[:])
         ones = held.tile([P, P], F32, name="ones")
         nc.vector.memset(ones[:], 1.0)
-
-        w1_sb = held.tile([D, M], BF16, name="w1_sb")
-        nc.scalar.dma_start(w1_sb[:], w1)
-        w2_sb = held.tile([P, M // P, Q], BF16, name="w2_sb")
-        nc.gpsimd.dma_start(w2_sb[:], w2.rearrange("(b p) q -> p b q", p=P))
-        b1_sb = held.tile([P, M // P], F32, name="b1_sb")
-        b2_sb = held.tile([P, Q // P], F32, name="b2_sb")
-        with nc.allow_non_contiguous_dma(reason="256 floats, one to a partition"):
-            nc.gpsimd.dma_start(b1_sb[:], b1.rearrange("(b p) o -> p (b o)", p=P))
-            nc.gpsimd.dma_start(b2_sb[:], b2.rearrange("(b p) o -> p (b o)", p=P))
+        table_warmer = held.tile([P, 1], F32, name="table_warmer")
+        nc.scalar.activation(table_warmer[:], ones[:, 0:1], ACT.Abs_reciprocal_sqrt)
 
         window = held.tile([D, S], BF16, name="window")
         for h in range(2):
@@ -103,4 +104,5 @@ def tile_npmlphead_kernel(tc, table, w1, b1, w2, b2, offs, out):
             nc.vector.scalar_tensor_tensor(
                 result[:], y_ps[qb][:], b2_sb[:, qb : qb + 1], inv_norm[:], op0=ALU.add, op1=ALU.mult
             )
-            nc.sync.dma_start(out[qb * P : (qb + 1) * P, :], result[:])
+            store_queue = nc.sync if qb == 0 else nc.scalar
+            store_queue.dma_start(out[qb * P : (qb + 1) * P, :], result[:])

@@ -11,30 +11,40 @@ ALU = mybir.AluOpType
 FLOPS = 2 * N * (D * M + M * Q)
 BYTES = 2 * N * D + 2 * D * M + 4 * M + 2 * M * Q + 4 * Q + 2 * P * (N // 16) + 4 * Q * N
 
+CHUNKS = 4
+CHUNK_BLOCKS = S // P // CHUNKS
+CHUNK_ROWS = CHUNK_BLOCKS * P
+PIECES = 2
+COLS = N // PIECES
+MB = M // P
+QB = Q // P
+
 
 def tile_npmlphead_kernel(tc, table, w1, b1, w2, b2, offs, out):
     nc = tc.nc
-    row_blocks = S // P
-    half_blocks = row_blocks // 2
     with (
         tc.tile_pool(name="held", bufs=1) as held,
-        tc.psum_pool(name="psum", bufs=1) as psum,
+        tc.psum_pool(name="y_banks", bufs=1) as y_banks,
+        tc.psum_pool(name="work", bufs=4) as work,
     ):
         blocked = table.rearrange("(b p) d -> p b d", p=P)
-        rows = [held.tile([P, half_blocks, D], BF16, name=f"rows{h}") for h in range(2)]
-        nc.sync.dma_start(rows[0][:], blocked[:, 0:half_blocks, :])
-        nc.scalar.dma_start(rows[1][:], blocked[:, half_blocks:row_blocks, :])
+        rows = []
+        for c in range(CHUNKS):
+            rows_c = held.tile([P, CHUNK_BLOCKS, D], BF16, name=f"rows{c}")
+            load_queue = nc.sync if c % 2 == 0 else nc.scalar
+            load_queue.dma_start(rows_c[:], blocked[:, c * CHUNK_BLOCKS : (c + 1) * CHUNK_BLOCKS, :])
+            rows.append(rows_c)
 
         offsets = held.tile([P, N // 16], U16, name="offsets")
         nc.sync.dma_start(offsets[:], offs)
         w1_sb = held.tile([D, M], BF16, name="w1_sb")
         nc.scalar.dma_start(w1_sb[:], w1)
-        b1_sb = held.tile([P, M // P], F32, name="b1_sb")
-        b2_sb = held.tile([P, Q // P], F32, name="b2_sb")
+        b1_sb = held.tile([P, MB], F32, name="b1_sb")
+        b2_sb = held.tile([P, QB], F32, name="b2_sb")
         with nc.allow_non_contiguous_dma(reason="256 floats, one to a partition"):
             nc.sync.dma_start(b1_sb[:], b1.rearrange("(b p) o -> p (b o)", p=P))
             nc.sync.dma_start(b2_sb[:], b2.rearrange("(b p) o -> p (b o)", p=P))
-        w2_sb = held.tile([P, M // P, Q], BF16, name="w2_sb")
+        w2_sb = held.tile([P, MB, Q], BF16, name="w2_sb")
         nc.scalar.dma_start(w2_sb[:], w2.rearrange("(b p) q -> p b q", p=P))
 
         identity = held.tile([P, P], BF16, name="identity")
@@ -45,64 +55,71 @@ def tile_npmlphead_kernel(tc, table, w1, b1, w2, b2, offs, out):
         nc.scalar.activation(table_warmer[:], ones[:, 0:1], ACT.Abs_reciprocal_sqrt)
 
         window = held.tile([D, S], BF16, name="window")
-        for h in range(2):
-            flipped = psum.tile([D, half_blocks * P], BF16, name=f"flipped{h}")
-            for k in range(half_blocks):
-                nc.tensor.transpose(flipped[:, k * P : (k + 1) * P], rows[h][:, k, :], identity[:])
-            half = window[:, h * half_blocks * P : (h + 1) * half_blocks * P]
-            if h == 0:
-                nc.vector.tensor_copy(half, flipped[:])
+        for c in range(CHUNKS):
+            flipped = work.tile([D, CHUNK_ROWS], BF16, name=f"flipped{c}", tag="work")
+            for k in range(CHUNK_BLOCKS):
+                nc.tensor.transpose(flipped[:, k * P : (k + 1) * P], rows[c][:, k, :], identity[:])
+            window_part = window[:, c * CHUNK_ROWS : (c + 1) * CHUNK_ROWS]
+            if c % 2 == 0:
+                nc.vector.tensor_copy(window_part, flipped[:])
             else:
-                nc.scalar.copy(half, flipped[:])
+                nc.scalar.copy(window_part, flipped[:])
 
         hidden = []
-        for mb in range(M // P):
-            hidden_ps = psum.tile([P, N], F32, name=f"hidden_ps{mb}")
-            nc.tensor.matmul(
-                hidden_ps[:],
-                w1_sb[:, mb * P : (mb + 1) * P],
-                window[:].indirect(offsets[:]),
-                start=True,
-                stop=True,
-            )
-            hidden_mb = held.tile([P, N], BF16, name=f"hidden{mb}")
-            if mb == 0:
-                nc.scalar.activation(hidden_mb[:], hidden_ps[:], ACT.Relu, bias=b1_sb[:, mb : mb + 1])
-            else:
-                nc.vector.tensor_scalar(
-                    hidden_mb[:], hidden_ps[:], b1_sb[:, mb : mb + 1], 0.0, op0=ALU.add, op1=ALU.max
+        for c in range(PIECES):
+            hidden_c = []
+            for mb in range(MB):
+                hidden_ps = work.tile([P, COLS], F32, name=f"hidden_ps{c}{mb}", tag="work")
+                nc.tensor.matmul(
+                    hidden_ps[:],
+                    w1_sb[:, mb * P : (mb + 1) * P],
+                    window[:].indirect(offsets[:, c * (COLS // 16) : (c + 1) * (COLS // 16)]),
+                    start=True,
+                    stop=True,
                 )
-            hidden.append(hidden_mb)
+                hidden_mb = held.tile([P, COLS], BF16, name=f"hidden{c}{mb}")
+                if mb == 0:
+                    nc.scalar.activation(hidden_mb[:], hidden_ps[:], ACT.Relu, bias=b1_sb[:, mb : mb + 1])
+                else:
+                    nc.vector.tensor_scalar(
+                        hidden_mb[:], hidden_ps[:], b1_sb[:, mb : mb + 1], 0.0, op0=ALU.add, op1=ALU.max
+                    )
+                hidden_c.append(hidden_mb)
+            hidden.append(hidden_c)
 
         y_ps = []
         squares = []
-        for qb in range(Q // P):
-            y_qb = psum.tile([P, N], F32, name=f"y_ps{qb}")
-            for mb in range(M // P):
+        for c in range(PIECES):
+            y_c = []
+            squares_c = []
+            for qb in range(QB):
+                y_qb = y_banks.tile([P, COLS], F32, name=f"y_ps{c}{qb}")
+                for mb in range(MB):
+                    nc.tensor.matmul(
+                        y_qb[:],
+                        w2_sb[:, mb, qb * P : (qb + 1) * P],
+                        hidden[c][mb][:],
+                        start=(mb == 0),
+                        stop=(mb == MB - 1),
+                    )
+                square_qb = held.tile([P, COLS], F32, name=f"square{c}{qb}")
+                nc.scalar.activation(square_qb[:], y_qb[:], ACT.Square, bias=b2_sb[:, qb : qb + 1])
+                y_c.append(y_qb)
+                squares_c.append(square_qb)
+            y_ps.append(y_c)
+            squares.append(squares_c)
+
+        for c in range(PIECES):
+            sumsq_ps = work.tile([P, COLS], F32, name=f"sumsq_ps{c}", tag="work")
+            for qb in range(QB):
                 nc.tensor.matmul(
-                    y_qb[:],
-                    w2_sb[:, mb, qb * P : (qb + 1) * P],
-                    hidden[mb][:],
-                    start=(mb == 0),
-                    stop=(mb == M // P - 1),
+                    sumsq_ps[:], ones[:], squares[c][qb][:], start=(qb == 0), stop=(qb == QB - 1)
                 )
-            square_qb = held.tile([P, N], F32, name=f"square{qb}")
-            nc.scalar.activation(square_qb[:], y_qb[:], ACT.Square, bias=b2_sb[:, qb : qb + 1])
-            y_ps.append(y_qb)
-            squares.append(square_qb)
-
-        sumsq_ps = psum.tile([P, N], F32, name="sumsq_ps")
-        for qb in range(Q // P):
-            nc.tensor.matmul(
-                sumsq_ps[:], ones[:], squares[qb][:], start=(qb == 0), stop=(qb == Q // P - 1)
-            )
-        inv_norm = held.tile([P, N], F32, name="inv_norm")
-        nc.scalar.activation(inv_norm[:], sumsq_ps[:], ACT.Abs_reciprocal_sqrt)
-
-        for qb in range(Q // P):
-            result = held.tile([P, N], F32, name=f"result{qb}")
-            nc.vector.scalar_tensor_tensor(
-                result[:], y_ps[qb][:], b2_sb[:, qb : qb + 1], inv_norm[:], op0=ALU.add, op1=ALU.mult
-            )
-            store_queue = nc.sync if qb == 0 else nc.scalar
-            store_queue.dma_start(out[qb * P : (qb + 1) * P, :], result[:])
+            inv_norm = held.tile([P, COLS], F32, name=f"inv_norm{c}")
+            nc.scalar.activation(inv_norm[:], sumsq_ps[:], ACT.Abs_reciprocal_sqrt)
+            for qb in range(QB):
+                result = held.tile([P, COLS], F32, name=f"result{c}{qb}")
+                nc.vector.scalar_tensor_tensor(
+                    result[:], y_ps[c][qb][:], b2_sb[:, qb : qb + 1], inv_norm[:], op0=ALU.add, op1=ALU.mult
+                )
+                nc.sync.dma_start(out[qb * P : (qb + 1) * P, c * COLS : (c + 1) * COLS], result[:])

@@ -18,6 +18,13 @@ PIECES = 2
 COLS = N // PIECES
 MB = M // P
 QB = Q // P
+WARM_START = 8
+WARM_PAIR = 3
+
+
+def keep_tensor_engine_busy(nc, bank, scratch, times):
+    for i in range(times):
+        nc.tensor.matmul(bank[:], scratch[:, 0:P], scratch[:], start=True, stop=True)
 
 
 def tile_npmlphead_kernel(tc, table, w1, b1, w2, b2, offs, out):
@@ -47,6 +54,11 @@ def tile_npmlphead_kernel(tc, table, w1, b1, w2, b2, offs, out):
         w2_sb = held.tile([P, MB, Q], BF16, name="w2_sb")
         nc.scalar.dma_start(w2_sb[:], w2.rearrange("(b p) q -> p b q", p=P))
 
+        y_ps = [[y_banks.tile([P, COLS], F32, name=f"y_ps{c}{qb}") for qb in range(QB)] for c in range(PIECES)]
+        scratch = held.tile([P, COLS], BF16, name="scratch")
+        nc.vector.memset(scratch[:], 1.0)
+        keep_tensor_engine_busy(nc, y_ps[0][0], scratch, WARM_START)
+
         identity = held.tile([P, P], BF16, name="identity")
         make_identity(nc, identity[:])
         ones = held.tile([P, P], F32, name="ones")
@@ -64,6 +76,7 @@ def tile_npmlphead_kernel(tc, table, w1, b1, w2, b2, offs, out):
                 nc.vector.tensor_copy(window_part, flipped[:])
             else:
                 nc.scalar.copy(window_part, flipped[:])
+                keep_tensor_engine_busy(nc, y_ps[0][0], scratch, WARM_PAIR)
 
         hidden = []
         for c in range(PIECES):
@@ -87,13 +100,11 @@ def tile_npmlphead_kernel(tc, table, w1, b1, w2, b2, offs, out):
                 hidden_c.append(hidden_mb)
             hidden.append(hidden_c)
 
-        y_ps = []
         squares = []
         for c in range(PIECES):
-            y_c = []
             squares_c = []
             for qb in range(QB):
-                y_qb = y_banks.tile([P, COLS], F32, name=f"y_ps{c}{qb}")
+                y_qb = y_ps[c][qb]
                 for mb in range(MB):
                     nc.tensor.matmul(
                         y_qb[:],
@@ -104,9 +115,7 @@ def tile_npmlphead_kernel(tc, table, w1, b1, w2, b2, offs, out):
                     )
                 square_qb = held.tile([P, COLS], F32, name=f"square{c}{qb}")
                 nc.scalar.activation(square_qb[:], y_qb[:], ACT.Square, bias=b2_sb[:, qb : qb + 1])
-                y_c.append(y_qb)
                 squares_c.append(square_qb)
-            y_ps.append(y_c)
             squares.append(squares_c)
 
         for c in range(PIECES):

@@ -18,13 +18,6 @@ PIECES = 2
 COLS = N // PIECES
 MB = M // P
 QB = Q // P
-WARM_START = 8
-WARM_PAIR = 3
-
-
-def keep_tensor_engine_busy(nc, bank, scratch, times):
-    for i in range(times):
-        nc.tensor.matmul(bank[:], scratch[:, 0:P], scratch[:], start=True, stop=True)
 
 
 def tile_npmlphead_kernel(tc, table, w1, b1, w2, b2, offs, out):
@@ -54,11 +47,6 @@ def tile_npmlphead_kernel(tc, table, w1, b1, w2, b2, offs, out):
         w2_sb = held.tile([P, MB, Q], BF16, name="w2_sb")
         nc.scalar.dma_start(w2_sb[:], w2.rearrange("(b p) q -> p b q", p=P))
 
-        y_ps = [[y_banks.tile([P, COLS], F32, name=f"y_ps{c}{qb}") for qb in range(QB)] for c in range(PIECES)]
-        scratch = held.tile([P, COLS], BF16, name="scratch")
-        nc.vector.memset(scratch[:], 1.0)
-        keep_tensor_engine_busy(nc, y_ps[0][0], scratch, WARM_START)
-
         identity = held.tile([P, P], BF16, name="identity")
         make_identity(nc, identity[:])
         ones = held.tile([P, P], F32, name="ones")
@@ -76,7 +64,6 @@ def tile_npmlphead_kernel(tc, table, w1, b1, w2, b2, offs, out):
                 nc.vector.tensor_copy(window_part, flipped[:])
             else:
                 nc.scalar.copy(window_part, flipped[:])
-                keep_tensor_engine_busy(nc, y_ps[0][0], scratch, WARM_PAIR)
 
         hidden = []
         for c in range(PIECES):
@@ -100,11 +87,13 @@ def tile_npmlphead_kernel(tc, table, w1, b1, w2, b2, offs, out):
                 hidden_c.append(hidden_mb)
             hidden.append(hidden_c)
 
+        y_ps = []
         squares = []
         for c in range(PIECES):
+            y_c = []
             squares_c = []
             for qb in range(QB):
-                y_qb = y_ps[c][qb]
+                y_qb = y_banks.tile([P, COLS], F32, name=f"y_ps{c}{qb}")
                 for mb in range(MB):
                     nc.tensor.matmul(
                         y_qb[:],
@@ -115,15 +104,16 @@ def tile_npmlphead_kernel(tc, table, w1, b1, w2, b2, offs, out):
                     )
                 square_qb = held.tile([P, COLS], F32, name=f"square{c}{qb}")
                 nc.scalar.activation(square_qb[:], y_qb[:], ACT.Square, bias=b2_sb[:, qb : qb + 1])
+                y_c.append(y_qb)
                 squares_c.append(square_qb)
-            squares.append(squares_c)
+            y_ps.append(y_c)
+            both_blocks = held.tile([P, COLS], F32, name=f"both_blocks{c}")
+            nc.vector.tensor_tensor(both_blocks[:], squares_c[0][:], squares_c[1][:], ALU.add)
+            squares.append(both_blocks)
 
         for c in range(PIECES):
             sumsq_ps = work.tile([P, COLS], F32, name=f"sumsq_ps{c}", tag="work")
-            for qb in range(QB):
-                nc.tensor.matmul(
-                    sumsq_ps[:], ones[:], squares[c][qb][:], start=(qb == 0), stop=(qb == QB - 1)
-                )
+            nc.tensor.matmul(sumsq_ps[:], ones[:], squares[c][:], start=True, stop=True)
             inv_norm = held.tile([P, COLS], F32, name=f"inv_norm{c}")
             nc.scalar.activation(inv_norm[:], sumsq_ps[:], ACT.Abs_reciprocal_sqrt)
             for qb in range(QB):

@@ -18,6 +18,13 @@ PIECES = 2
 COLS = N // PIECES
 MB = M // P
 QB = Q // P
+WARM_START = 6
+WARM_PAIR = 1
+
+
+def keep_tensor_engine_busy(nc, bank, scratch, times):
+    for i in range(times):
+        nc.tensor.matmul(bank[:], scratch[:, 0:P], scratch[:], start=True, stop=True)
 
 
 def tile_npmlphead_kernel(tc, table, w1, b1, w2, b2, offs, out):
@@ -47,6 +54,11 @@ def tile_npmlphead_kernel(tc, table, w1, b1, w2, b2, offs, out):
         w2_sb = held.tile([P, MB, Q], BF16, name="w2_sb")
         nc.scalar.dma_start(w2_sb[:], w2.rearrange("(b p) q -> p b q", p=P))
 
+        y_ps = [[y_banks.tile([P, COLS], F32, name=f"y_ps{c}{qb}") for qb in range(QB)] for c in range(PIECES)]
+        scratch = held.tile([P, COLS], BF16, name="scratch")
+        nc.vector.memset(scratch[:], 1.0)
+        keep_tensor_engine_busy(nc, y_ps[0][0], scratch, WARM_START)
+
         identity = held.tile([P, P], BF16, name="identity")
         make_identity(nc, identity[:])
         ones = held.tile([P, P], F32, name="ones")
@@ -64,6 +76,7 @@ def tile_npmlphead_kernel(tc, table, w1, b1, w2, b2, offs, out):
                 nc.vector.tensor_copy(window_part, flipped[:])
             else:
                 nc.scalar.copy(window_part, flipped[:])
+                keep_tensor_engine_busy(nc, y_ps[0][0], scratch, WARM_PAIR)
 
         hidden = []
         for c in range(PIECES):
@@ -87,13 +100,11 @@ def tile_npmlphead_kernel(tc, table, w1, b1, w2, b2, offs, out):
                 hidden_c.append(hidden_mb)
             hidden.append(hidden_c)
 
-        y_ps = []
         squares = []
         for c in range(PIECES):
-            y_c = []
             squares_c = []
             for qb in range(QB):
-                y_qb = y_banks.tile([P, COLS], F32, name=f"y_ps{c}{qb}")
+                y_qb = y_ps[c][qb]
                 for mb in range(MB):
                     nc.tensor.matmul(
                         y_qb[:],
@@ -104,9 +115,7 @@ def tile_npmlphead_kernel(tc, table, w1, b1, w2, b2, offs, out):
                     )
                 square_qb = held.tile([P, COLS], F32, name=f"square{c}{qb}")
                 nc.scalar.activation(square_qb[:], y_qb[:], ACT.Square, bias=b2_sb[:, qb : qb + 1])
-                y_c.append(y_qb)
                 squares_c.append(square_qb)
-            y_ps.append(y_c)
             both_blocks = held.tile([P, COLS], F32, name=f"both_blocks{c}")
             nc.vector.tensor_tensor(both_blocks[:], squares_c[0][:], squares_c[1][:], ALU.add)
             squares.append(both_blocks)

@@ -14,8 +14,10 @@ BYTES = 2 * N * D + 2 * D * M + 4 * M + 2 * M * Q + 4 * Q + 2 * P * (N // 16) + 
 CHUNKS = 4
 CHUNK_BLOCKS = S // P // CHUNKS
 CHUNK_ROWS = CHUNK_BLOCKS * P
-PIECES = 2
-COLS = N // PIECES
+PIECE_COLS = (192, 192, 128)
+PIECE_START = (0, 192, 384)
+PIECES = len(PIECE_COLS)
+WARM_COLS = 256
 MB = M // P
 QB = Q // P
 WARM_START = 6
@@ -29,11 +31,7 @@ def keep_tensor_engine_busy(nc, bank, scratch, times):
 
 def tile_npmlphead_kernel(tc, table, w1, b1, w2, b2, offs, out):
     nc = tc.nc
-    with (
-        tc.tile_pool(name="held", bufs=1) as held,
-        tc.psum_pool(name="y_banks", bufs=1) as y_banks,
-        tc.psum_pool(name="work", bufs=4) as work,
-    ):
+    with tc.tile_pool(name="held", bufs=1) as held:
         blocked = table.rearrange("(b p) d -> p b d", p=P)
         rows = []
         for c in range(CHUNKS):
@@ -54,80 +52,94 @@ def tile_npmlphead_kernel(tc, table, w1, b1, w2, b2, offs, out):
         w2_sb = held.tile([P, MB, Q], BF16, name="w2_sb")
         nc.scalar.dma_start(w2_sb[:], w2.rearrange("(b p) q -> p b q", p=P))
 
-        y_ps = [[y_banks.tile([P, COLS], F32, name=f"y_ps{c}{qb}") for qb in range(QB)] for c in range(PIECES)]
-        scratch = held.tile([P, COLS], BF16, name="scratch")
-        nc.vector.memset(scratch[:], 1.0)
-        keep_tensor_engine_busy(nc, y_ps[0][0], scratch, WARM_START)
-
-        identity = held.tile([P, P], BF16, name="identity")
-        make_identity(nc, identity[:])
-        ones = held.tile([P, P], F32, name="ones")
-        nc.vector.memset(ones[:], 1.0)
-        table_warmer = held.tile([P, 1], F32, name="table_warmer")
-        nc.scalar.activation(table_warmer[:], ones[:, 0:1], ACT.Abs_reciprocal_sqrt)
-
         window = held.tile([D, S], BF16, name="window")
-        for c in range(CHUNKS):
-            flipped = work.tile([D, CHUNK_ROWS], BF16, name=f"flipped{c}", tag="work")
-            for k in range(CHUNK_BLOCKS):
-                nc.tensor.transpose(flipped[:, k * P : (k + 1) * P], rows[c][:, k, :], identity[:])
-            window_part = window[:, c * CHUNK_ROWS : (c + 1) * CHUNK_ROWS]
-            if c % 2 == 0:
-                nc.vector.tensor_copy(window_part, flipped[:])
-            else:
-                nc.scalar.copy(window_part, flipped[:])
-                keep_tensor_engine_busy(nc, y_ps[0][0], scratch, WARM_PAIR)
+        ones = held.tile([P, P], F32, name="ones")
 
-        hidden = []
-        for c in range(PIECES):
-            hidden_c = []
-            for mb in range(MB):
-                hidden_ps = work.tile([P, COLS], F32, name=f"hidden_ps{c}{mb}", tag="work")
-                nc.tensor.matmul(
-                    hidden_ps[:],
-                    w1_sb[:, mb * P : (mb + 1) * P],
-                    window[:].indirect(offsets[:, c * (COLS // 16) : (c + 1) * (COLS // 16)]),
-                    start=True,
-                    stop=True,
-                )
-                hidden_mb = held.tile([P, COLS], BF16, name=f"hidden{c}{mb}")
-                if mb == 0:
-                    nc.scalar.activation(hidden_mb[:], hidden_ps[:], ACT.Relu, bias=b1_sb[:, mb : mb + 1])
+        with tc.psum_pool(name="flip_banks", bufs=1) as flip_banks:
+            warm_bank = flip_banks.tile([P, WARM_COLS], F32, name="warm_bank")
+            scratch = held.tile([P, WARM_COLS], BF16, name="scratch")
+            nc.vector.memset(scratch[:], 1.0)
+            keep_tensor_engine_busy(nc, warm_bank, scratch, WARM_START)
+
+            identity = held.tile([P, P], BF16, name="identity")
+            make_identity(nc, identity[:])
+            nc.vector.memset(ones[:], 1.0)
+            table_warmer = held.tile([P, 1], F32, name="table_warmer")
+            nc.scalar.activation(table_warmer[:], ones[:, 0:1], ACT.Abs_reciprocal_sqrt)
+
+            for c in range(CHUNKS):
+                flipped = flip_banks.tile([D, CHUNK_ROWS], BF16, name=f"flipped{c}")
+                for k in range(CHUNK_BLOCKS):
+                    nc.tensor.transpose(flipped[:, k * P : (k + 1) * P], rows[c][:, k, :], identity[:])
+                window_part = window[:, c * CHUNK_ROWS : (c + 1) * CHUNK_ROWS]
+                if c % 2 == 0:
+                    nc.vector.tensor_copy(window_part, flipped[:])
                 else:
-                    nc.vector.tensor_scalar(
-                        hidden_mb[:], hidden_ps[:], b1_sb[:, mb : mb + 1], 0.0, op0=ALU.add, op1=ALU.max
-                    )
-                hidden_c.append(hidden_mb)
-            hidden.append(hidden_c)
+                    nc.scalar.copy(window_part, flipped[:])
+                    keep_tensor_engine_busy(nc, warm_bank, scratch, WARM_PAIR)
 
-        squares = []
-        for c in range(PIECES):
-            squares_c = []
-            for qb in range(QB):
-                y_qb = y_ps[c][qb]
+        with (
+            tc.psum_pool(name="products", bufs=1) as products,
+            tc.psum_pool(name="sums", bufs=2) as sums,
+        ):
+            product = [
+                [products.tile([P, PIECE_COLS[c]], F32, name=f"product{c}{b}") for b in range(MB)]
+                for c in range(PIECES)
+            ]
+
+            hidden = []
+            for c in range(PIECES):
+                cols, first = PIECE_COLS[c], PIECE_START[c]
+                hidden_c = []
                 for mb in range(MB):
                     nc.tensor.matmul(
-                        y_qb[:],
-                        w2_sb[:, mb, qb * P : (qb + 1) * P],
-                        hidden[c][mb][:],
-                        start=(mb == 0),
-                        stop=(mb == MB - 1),
+                        product[c][mb][:],
+                        w1_sb[:, mb * P : (mb + 1) * P],
+                        window[:].indirect(offsets[:, first // 16 : (first + cols) // 16]),
+                        start=True,
+                        stop=True,
                     )
-                square_qb = held.tile([P, COLS], F32, name=f"square{c}{qb}")
-                nc.scalar.activation(square_qb[:], y_qb[:], ACT.Square, bias=b2_sb[:, qb : qb + 1])
-                squares_c.append(square_qb)
-            both_blocks = held.tile([P, COLS], F32, name=f"both_blocks{c}")
-            nc.vector.tensor_tensor(both_blocks[:], squares_c[0][:], squares_c[1][:], ALU.add)
-            squares.append(both_blocks)
+                    hidden_mb = held.tile([P, cols], BF16, name=f"hidden{c}{mb}")
+                    if mb == 0:
+                        nc.scalar.activation(
+                            hidden_mb[:], product[c][mb][:], ACT.Relu, bias=b1_sb[:, mb : mb + 1]
+                        )
+                    else:
+                        nc.vector.tensor_scalar(
+                            hidden_mb[:], product[c][mb][:], b1_sb[:, mb : mb + 1], 0.0, op0=ALU.add, op1=ALU.max
+                        )
+                    hidden_c.append(hidden_mb)
+                hidden.append(hidden_c)
 
-        for c in range(PIECES):
-            sumsq_ps = work.tile([P, COLS], F32, name=f"sumsq_ps{c}", tag="work")
-            nc.tensor.matmul(sumsq_ps[:], ones[:], squares[c][:], start=True, stop=True)
-            inv_norm = held.tile([P, COLS], F32, name=f"inv_norm{c}")
-            nc.scalar.activation(inv_norm[:], sumsq_ps[:], ACT.Abs_reciprocal_sqrt)
-            for qb in range(QB):
-                result = held.tile([P, COLS], F32, name=f"result{c}{qb}")
-                nc.vector.scalar_tensor_tensor(
-                    result[:], y_ps[c][qb][:], b2_sb[:, qb : qb + 1], inv_norm[:], op0=ALU.add, op1=ALU.mult
-                )
-                nc.sync.dma_start(out[qb * P : (qb + 1) * P, c * COLS : (c + 1) * COLS], result[:])
+            squares = []
+            for c in range(PIECES):
+                cols = PIECE_COLS[c]
+                squares_c = []
+                for qb in range(QB):
+                    for mb in range(MB):
+                        nc.tensor.matmul(
+                            product[c][qb][:],
+                            w2_sb[:, mb, qb * P : (qb + 1) * P],
+                            hidden[c][mb][:],
+                            start=(mb == 0),
+                            stop=(mb == MB - 1),
+                        )
+                    square_qb = held.tile([P, cols], F32, name=f"square{c}{qb}")
+                    nc.scalar.activation(square_qb[:], product[c][qb][:], ACT.Square, bias=b2_sb[:, qb : qb + 1])
+                    squares_c.append(square_qb)
+                both_blocks = held.tile([P, cols], F32, name=f"both_blocks{c}")
+                nc.vector.tensor_tensor(both_blocks[:], squares_c[0][:], squares_c[1][:], ALU.add)
+                squares.append(both_blocks)
+
+            for c in range(PIECES):
+                cols, first = PIECE_COLS[c], PIECE_START[c]
+                sumsq_ps = sums.tile([P, cols], F32, name=f"sumsq_ps{c}", tag="sums")
+                nc.tensor.matmul(sumsq_ps[:], ones[:], squares[c][:], start=True, stop=True)
+                inv_norm = held.tile([P, cols], F32, name=f"inv_norm{c}")
+                nc.scalar.activation(inv_norm[:], sumsq_ps[:], ACT.Abs_reciprocal_sqrt)
+                for qb in range(QB):
+                    result = held.tile([P, cols], F32, name=f"result{c}{qb}")
+                    nc.vector.scalar_tensor_tensor(
+                        result[:], product[c][qb][:], b2_sb[:, qb : qb + 1], inv_norm[:], op0=ALU.add, op1=ALU.mult
+                    )
+                    nc.sync.dma_start(out[qb * P : (qb + 1) * P, first : first + cols], result[:])

@@ -14,8 +14,8 @@ BYTES = 2 * N * D + 2 * D * M + 4 * M + 2 * M * Q + 4 * Q + 2 * P * (N // 16) + 
 CHUNKS = 4
 CHUNK_BLOCKS = S // P // CHUNKS
 CHUNK_ROWS = CHUNK_BLOCKS * P
-PIECE_COLS = (192, 192, 128)
-PIECE_START = (0, 192, 384)
+PIECE_COLS = (128, 128, 128, 128)
+PIECE_START = (0, 128, 256, 384)
 PIECES = len(PIECE_COLS)
 WARM_COLS = 256
 MB = M // P
@@ -52,6 +52,7 @@ def tile_npmlphead_kernel(tc, table, w1, b1, w2, b2, offs, out):
         w2_sb = held.tile([P, MB, Q], BF16, name="w2_sb")
         nc.scalar.dma_start(w2_sb[:], w2.rearrange("(b p) q -> p b q", p=P))
 
+        out_blocked = out.rearrange("(b p) j -> p b j", p=P)
         window = held.tile([D, S], BF16, name="window")
         ones = held.tile([P, P], F32, name="ones")
 
@@ -78,22 +79,16 @@ def tile_npmlphead_kernel(tc, table, w1, b1, w2, b2, offs, out):
                     nc.scalar.copy(window_part, flipped[:])
                     keep_tensor_engine_busy(nc, warm_bank, scratch, WARM_PAIR)
 
-        with (
-            tc.psum_pool(name="products", bufs=1) as products,
-            tc.psum_pool(name="sums", bufs=2) as sums,
-        ):
-            product = [
-                [products.tile([P, PIECE_COLS[c]], F32, name=f"product{c}{b}") for b in range(MB)]
-                for c in range(PIECES)
-            ]
+        with tc.psum_pool(name="banks", bufs=8) as banks:
 
             hidden = []
             for c in range(PIECES):
                 cols, first = PIECE_COLS[c], PIECE_START[c]
                 hidden_c = []
                 for mb in range(MB):
+                    hidden_ps = banks.tile([P, cols], F32, name=f"hidden_ps{c}{mb}", tag="bank")
                     nc.tensor.matmul(
-                        product[c][mb][:],
+                        hidden_ps[:],
                         w1_sb[:, mb * P : (mb + 1) * P],
                         window[:].indirect(offsets[:, first // 16 : (first + cols) // 16]),
                         start=True,
@@ -101,31 +96,33 @@ def tile_npmlphead_kernel(tc, table, w1, b1, w2, b2, offs, out):
                     )
                     hidden_mb = held.tile([P, cols], BF16, name=f"hidden{c}{mb}")
                     if mb == 0:
-                        nc.scalar.activation(
-                            hidden_mb[:], product[c][mb][:], ACT.Relu, bias=b1_sb[:, mb : mb + 1]
-                        )
+                        nc.scalar.activation(hidden_mb[:], hidden_ps[:], ACT.Relu, bias=b1_sb[:, mb : mb + 1])
                     else:
                         nc.vector.tensor_scalar(
-                            hidden_mb[:], product[c][mb][:], b1_sb[:, mb : mb + 1], 0.0, op0=ALU.add, op1=ALU.max
+                            hidden_mb[:], hidden_ps[:], b1_sb[:, mb : mb + 1], 0.0, op0=ALU.add, op1=ALU.max
                         )
                     hidden_c.append(hidden_mb)
                 hidden.append(hidden_c)
 
             squares = []
+            y_ps = []
             for c in range(PIECES):
                 cols = PIECE_COLS[c]
-                squares_c = []
+                y_c = banks.tile([P, QB, cols], F32, name=f"y_ps{c}", tag="bank")
+                y_ps.append(y_c)
                 for qb in range(QB):
                     for mb in range(MB):
                         nc.tensor.matmul(
-                            product[c][qb][:],
+                            y_ps[c][:, qb, :],
                             w2_sb[:, mb, qb * P : (qb + 1) * P],
                             hidden[c][mb][:],
                             start=(mb == 0),
                             stop=(mb == MB - 1),
                         )
+                squares_c = []
+                for qb in range(QB):
                     square_qb = held.tile([P, cols], F32, name=f"square{c}{qb}")
-                    nc.scalar.activation(square_qb[:], product[c][qb][:], ACT.Square, bias=b2_sb[:, qb : qb + 1])
+                    nc.scalar.activation(square_qb[:], y_ps[c][:, qb, :], ACT.Square, bias=b2_sb[:, qb : qb + 1])
                     squares_c.append(square_qb)
                 both_blocks = held.tile([P, cols], F32, name=f"both_blocks{c}")
                 nc.vector.tensor_tensor(both_blocks[:], squares_c[0][:], squares_c[1][:], ALU.add)
@@ -133,13 +130,13 @@ def tile_npmlphead_kernel(tc, table, w1, b1, w2, b2, offs, out):
 
             for c in range(PIECES):
                 cols, first = PIECE_COLS[c], PIECE_START[c]
-                sumsq_ps = sums.tile([P, cols], F32, name=f"sumsq_ps{c}", tag="sums")
+                sumsq_ps = banks.tile([P, cols], F32, name=f"sumsq_ps{c}", tag="bank")
                 nc.tensor.matmul(sumsq_ps[:], ones[:], squares[c][:], start=True, stop=True)
                 inv_norm = held.tile([P, cols], F32, name=f"inv_norm{c}")
                 nc.scalar.activation(inv_norm[:], sumsq_ps[:], ACT.Abs_reciprocal_sqrt)
+                result = held.tile([P, QB, cols], F32, name=f"result{c}")
                 for qb in range(QB):
-                    result = held.tile([P, cols], F32, name=f"result{c}{qb}")
                     nc.vector.scalar_tensor_tensor(
-                        result[:], product[c][qb][:], b2_sb[:, qb : qb + 1], inv_norm[:], op0=ALU.add, op1=ALU.mult
+                        result[:, qb, :], y_ps[c][:, qb, :], b2_sb[:, qb : qb + 1], inv_norm[:], op0=ALU.add, op1=ALU.mult
                     )
-                    nc.sync.dma_start(out[qb * P : (qb + 1) * P, first : first + cols], result[:])
+                nc.sync.dma_start(out_blocked[:, :, first : first + cols], result[:])

@@ -106,23 +106,25 @@ def tile_npmlphead_kernel(tc, table, w1, b1, w2, b2, offs, out):
 
             squares = []
             y_ps = []
+            sumsq_ps = []
             for c in range(PIECES):
                 cols = PIECE_COLS[c]
-                y_c = banks.tile([P, QB, cols], F32, name=f"y_ps{c}", tag="bank")
-                y_ps.append(y_c)
+                block0_and_sum = banks.tile([P, 2, cols], F32, name=f"block0_and_sum{c}", tag="bank")
+                block1 = banks.tile([P, cols], F32, name=f"block1{c}", tag="bank")
+                y_ps.append([block0_and_sum[:, 0, :], block1[:]])
+                sumsq_ps.append(block0_and_sum[:, 1, :])
+                squares_c = []
                 for qb in range(QB):
                     for mb in range(MB):
                         nc.tensor.matmul(
-                            y_ps[c][:, qb, :],
+                            y_ps[c][qb],
                             w2_sb[:, mb, qb * P : (qb + 1) * P],
                             hidden[c][mb][:],
                             start=(mb == 0),
                             stop=(mb == MB - 1),
                         )
-                squares_c = []
-                for qb in range(QB):
                     square_qb = held.tile([P, cols], F32, name=f"square{c}{qb}")
-                    nc.scalar.activation(square_qb[:], y_ps[c][:, qb, :], ACT.Square, bias=b2_sb[:, qb : qb + 1])
+                    nc.scalar.activation(square_qb[:], y_ps[c][qb], ACT.Square, bias=b2_sb[:, qb : qb + 1])
                     squares_c.append(square_qb)
                 both_blocks = held.tile([P, cols], F32, name=f"both_blocks{c}")
                 nc.vector.tensor_tensor(both_blocks[:], squares_c[0][:], squares_c[1][:], ALU.add)
@@ -130,13 +132,12 @@ def tile_npmlphead_kernel(tc, table, w1, b1, w2, b2, offs, out):
 
             for c in range(PIECES):
                 cols, first = PIECE_COLS[c], PIECE_START[c]
-                sumsq_ps = banks.tile([P, cols], F32, name=f"sumsq_ps{c}", tag="bank")
-                nc.tensor.matmul(sumsq_ps[:], ones[:], squares[c][:], start=True, stop=True)
+                nc.tensor.matmul(sumsq_ps[c], ones[:], squares[c][:], start=True, stop=True)
                 inv_norm = held.tile([P, cols], F32, name=f"inv_norm{c}")
-                nc.scalar.activation(inv_norm[:], sumsq_ps[:], ACT.Abs_reciprocal_sqrt)
+                nc.scalar.activation(inv_norm[:], sumsq_ps[c], ACT.Abs_reciprocal_sqrt)
                 result = held.tile([P, QB, cols], F32, name=f"result{c}")
                 for qb in range(QB):
                     nc.vector.scalar_tensor_tensor(
-                        result[:, qb, :], y_ps[c][:, qb, :], b2_sb[:, qb : qb + 1], inv_norm[:], op0=ALU.add, op1=ALU.mult
+                        result[:, qb, :], y_ps[c][qb], b2_sb[:, qb : qb + 1], inv_norm[:], op0=ALU.add, op1=ALU.mult
                     )
                 nc.sync.dma_start(out_blocked[:, :, first : first + cols], result[:])

@@ -140,4 +140,8 @@ def tile_npmlphead_kernel(tc, table, w1, b1, w2, b2, offs, out):
                     nc.vector.scalar_tensor_tensor(
                         result[:, qb, :], y_ps[c][qb], b2_sb[:, qb : qb + 1], inv_norm[:], op0=ALU.add, op1=ALU.mult
                     )
-                nc.sync.dma_start(out_blocked[:, :, first : first + cols], result[:])
+                    if c == PIECES - 1:
+                        store_queue = nc.sync if qb == 0 else nc.scalar
+                        store_queue.dma_start(out_blocked[:, qb, first : first + cols], result[:, qb, :])
+                if c < PIECES - 1:
+                    nc.sync.dma_start(out_blocked[:, :, first : first + cols], result[:])

@@ -141,7 +141,6 @@ def tile_npmlphead_kernel(tc, table, w1, b1, w2, b2, offs, out):
                         result[:, qb, :], y_ps[c][qb], b2_sb[:, qb : qb + 1], inv_norm[:], op0=ALU.add, op1=ALU.mult
                     )
                     if c == PIECES - 1:
-                        store_queue = nc.sync if qb == 0 else nc.scalar
-                        store_queue.dma_start(out_blocked[:, qb, first : first + cols], result[:, qb, :])
+                        nc.sync.dma_start(out_blocked[:, qb, first : first + cols], result[:, qb, :])
                 if c < PIECES - 1:
                     nc.sync.dma_start(out_blocked[:, :, first : first + cols], result[:])

@@ -20,8 +20,7 @@ PIECES = len(PIECE_COLS)
 WARM_COLS = 256
 MB = M // P
 QB = Q // P
-WARM_START = 6
-WARM_PAIR = 1
+WARM_START = 7
 
 
 def keep_tensor_engine_busy(nc, bank, scratch, times):
@@ -77,7 +76,6 @@ def tile_npmlphead_kernel(tc, table, w1, b1, w2, b2, offs, out):
                     nc.vector.tensor_copy(window_part, flipped[:])
                 else:
                     nc.scalar.copy(window_part, flipped[:])
-                    keep_tensor_engine_busy(nc, warm_bank, scratch, WARM_PAIR)
 
         with tc.psum_pool(name="banks", bufs=8) as banks:
 

@@ -21,11 +21,12 @@ WARM_COLS = 256
 MB = M // P
 QB = Q // P
 WARM_START = 7
+WARM_COPY = 2
 
 
-def keep_tensor_engine_busy(nc, bank, scratch, times):
+def keep_tensor_engine_busy(nc, bank, operand, times):
     for i in range(times):
-        nc.tensor.matmul(bank[:], scratch[:, 0:P], scratch[:], start=True, stop=True)
+        nc.tensor.matmul(bank[:], operand[:, 0:P], operand, start=True, stop=True)
 
 
 def tile_npmlphead_kernel(tc, table, w1, b1, w2, b2, offs, out):
@@ -59,7 +60,7 @@ def tile_npmlphead_kernel(tc, table, w1, b1, w2, b2, offs, out):
             warm_bank = flip_banks.tile([P, WARM_COLS], F32, name="warm_bank")
             scratch = held.tile([P, WARM_COLS], BF16, name="scratch")
             nc.vector.memset(scratch[:], 1.0)
-            keep_tensor_engine_busy(nc, warm_bank, scratch, WARM_START)
+            keep_tensor_engine_busy(nc, warm_bank, scratch[:], WARM_START)
 
             identity = held.tile([P, P], BF16, name="identity")
             make_identity(nc, identity[:])
@@ -76,6 +77,8 @@ def tile_npmlphead_kernel(tc, table, w1, b1, w2, b2, offs, out):
                     nc.vector.tensor_copy(window_part, flipped[:])
                 else:
                     nc.scalar.copy(window_part, flipped[:])
+            last_even = (CHUNKS - 2) * CHUNK_ROWS
+            keep_tensor_engine_busy(nc, warm_bank, window[:, last_even : last_even + WARM_COLS], WARM_COPY)
 
         with tc.psum_pool(name="banks", bufs=8) as banks:
 

@@ -56,8 +56,8 @@ def tile_npmlphead_kernel(tc, table, w1, b1, w2, b2, offs, out):
         window = held.tile([D, S], BF16, name="window")
         ones = held.tile([P, P], F32, name="ones")
 
-        with tc.psum_pool(name="flip_banks", bufs=1) as flip_banks:
-            warm_bank = flip_banks.tile([P, WARM_COLS], F32, name="warm_bank")
+        with tc.psum_pool(name="banks", bufs=8) as banks:
+            warm_bank = banks.tile([P, WARM_COLS], F32, name="warm_bank", tag="bank")
             scratch = held.tile([P, WARM_COLS], BF16, name="scratch")
             nc.vector.memset(scratch[:], 1.0)
             keep_tensor_engine_busy(nc, warm_bank, scratch[:], WARM_START)
@@ -69,7 +69,7 @@ def tile_npmlphead_kernel(tc, table, w1, b1, w2, b2, offs, out):
             nc.scalar.activation(table_warmer[:], ones[:, 0:1], ACT.Abs_reciprocal_sqrt)
 
             for c in range(CHUNKS):
-                flipped = flip_banks.tile([D, CHUNK_ROWS], BF16, name=f"flipped{c}")
+                flipped = banks.tile([D, CHUNK_ROWS], BF16, name=f"flipped{c}", tag="bank")
                 for k in range(CHUNK_BLOCKS):
                     nc.tensor.transpose(flipped[:, k * P : (k + 1) * P], rows[c][:, k, :], identity[:])
                 window_part = window[:, c * CHUNK_ROWS : (c + 1) * CHUNK_ROWS]
@@ -79,8 +79,6 @@ def tile_npmlphead_kernel(tc, table, w1, b1, w2, b2, offs, out):
                     nc.scalar.copy(window_part, flipped[:])
             last_even = (CHUNKS - 2) * CHUNK_ROWS
             keep_tensor_engine_busy(nc, warm_bank, window[:, last_even : last_even + WARM_COLS], WARM_COPY)
-
-        with tc.psum_pool(name="banks", bufs=8) as banks:
 
             hidden = []
             for c in range(PIECES):

@@ -77,8 +77,7 @@ def tile_npmlphead_kernel(tc, table, w1, b1, w2, b2, offs, out):
                     nc.vector.tensor_copy(window_part, flipped[:])
                 else:
                     nc.scalar.copy(window_part, flipped[:])
-            last_even = (CHUNKS - 2) * CHUNK_ROWS
-            keep_tensor_engine_busy(nc, warm_bank, window[:, last_even : last_even + WARM_COLS], WARM_COPY)
+            keep_tensor_engine_busy(nc, warm_bank, window[:, 0:WARM_COLS], WARM_COPY)
 
             hidden = []
             for c in range(PIECES):

@@ -124,13 +124,20 @@ def tile_npmlphead_kernel(tc, table, w1, b1, w2, b2, offs, out):
                     square_qb = held.tile([P, cols], F32, name=f"square{c}{qb}")
                     nc.scalar.activation(square_qb[:], y_ps[c][qb], ACT.Square, bias=b2_sb[:, qb : qb + 1])
                     squares_c.append(square_qb)
-                both_blocks = held.tile([P, cols], F32, name=f"both_blocks{c}")
-                nc.vector.tensor_tensor(both_blocks[:], squares_c[0][:], squares_c[1][:], ALU.add)
-                squares.append(both_blocks)
+                if c == 0:
+                    squares.append(squares_c)
+                else:
+                    both_blocks = held.tile([P, cols], F32, name=f"both_blocks{c}")
+                    nc.vector.tensor_tensor(both_blocks[:], squares_c[0][:], squares_c[1][:], ALU.add)
+                    squares.append([both_blocks])
 
             for c in range(PIECES):
                 cols, first = PIECE_COLS[c], PIECE_START[c]
-                nc.tensor.matmul(sumsq_ps[c], ones[:], squares[c][:], start=True, stop=True)
+                addends = squares[c]
+                for i in range(len(addends)):
+                    nc.tensor.matmul(
+                        sumsq_ps[c], ones[:], addends[i][:], start=(i == 0), stop=(i == len(addends) - 1)
+                    )
                 inv_norm = held.tile([P, cols], F32, name=f"inv_norm{c}")
                 nc.scalar.activation(inv_norm[:], sumsq_ps[c], ACT.Abs_reciprocal_sqrt)
                 result = held.tile([P, QB, cols], F32, name=f"result{c}")

@@ -124,7 +124,7 @@ def tile_npmlphead_kernel(tc, table, w1, b1, w2, b2, offs, out):
                     square_qb = held.tile([P, cols], F32, name=f"square{c}{qb}")
                     nc.scalar.activation(square_qb[:], y_ps[c][qb], ACT.Square, bias=b2_sb[:, qb : qb + 1])
                     squares_c.append(square_qb)
-                if c == 0:
+                if c in (0, PIECES - 1):
                     squares.append(squares_c)
                 else:
                     both_blocks = held.tile([P, cols], F32, name=f"both_blocks{c}")

import concourse.mybir as mybir
from concourse.masks import make_identity

S, D, M, Q, N = 1024, 128, 256, 256, 512
P = 128

BF16, F32, U16 = mybir.dt.bfloat16, mybir.dt.float32, mybir.dt.uint16
ACT = mybir.ActivationFunctionType
ALU = mybir.AluOpType

FLOPS = 2 * N * (D * M + M * Q)
BYTES = 2 * N * D + 2 * D * M + 4 * M + 2 * M * Q + 4 * Q + 2 * P * (N // 16) + 4 * Q * N

CHUNKS = 4
CHUNK_BLOCKS = S // P // CHUNKS
CHUNK_ROWS = CHUNK_BLOCKS * P
PIECE_COLS = (128, 128, 128, 128)
PIECE_START = (0, 128, 256, 384)
PIECES = len(PIECE_COLS)
WARM_COLS = 256
MB = M // P
QB = Q // P
WARM_START = 7
WARM_COPY = 2


def keep_tensor_engine_busy(nc, bank, operand, times):
    for i in range(times):
        nc.tensor.matmul(bank[:], operand[:, 0:P], operand, start=True, stop=True)


def tile_npmlphead_kernel(tc, table, w1, b1, w2, b2, offs, out):
    nc = tc.nc
    with tc.tile_pool(name="held", bufs=1) as held:
        blocked = table.rearrange("(b p) d -> p b d", p=P)
        rows = []
        for c in range(CHUNKS):
            rows_c = held.tile([P, CHUNK_BLOCKS, D], BF16, name=f"rows{c}")
            load_queue = nc.sync if c % 2 == 0 else nc.scalar
            load_queue.dma_start(rows_c[:], blocked[:, c * CHUNK_BLOCKS : (c + 1) * CHUNK_BLOCKS, :])
            rows.append(rows_c)

        offsets = held.tile([P, N // 16], U16, name="offsets")
        nc.sync.dma_start(offsets[:], offs)
        w1_sb = held.tile([D, M], BF16, name="w1_sb")
        nc.scalar.dma_start(w1_sb[:], w1)
        b1_sb = held.tile([P, MB], F32, name="b1_sb")
        b2_sb = held.tile([P, QB], F32, name="b2_sb")
        with nc.allow_non_contiguous_dma(reason="256 floats, one to a partition"):
            nc.sync.dma_start(b1_sb[:], b1.rearrange("(b p) o -> p (b o)", p=P))
            nc.sync.dma_start(b2_sb[:], b2.rearrange("(b p) o -> p (b o)", p=P))
        w2_sb = held.tile([P, MB, Q], BF16, name="w2_sb")
        nc.scalar.dma_start(w2_sb[:], w2.rearrange("(b p) q -> p b q", p=P))

        out_blocked = out.rearrange("(b p) j -> p b j", p=P)
        window = held.tile([D, S], BF16, name="window")
        ones = held.tile([P, P], F32, name="ones")

        with tc.psum_pool(name="banks", bufs=8) as banks:
            warm_bank = banks.tile([P, WARM_COLS], F32, name="warm_bank", tag="bank")
            scratch = held.tile([P, WARM_COLS], BF16, name="scratch")
            nc.vector.memset(scratch[:], 1.0)
            keep_tensor_engine_busy(nc, warm_bank, scratch[:], WARM_START)

            identity = held.tile([P, P], BF16, name="identity")
            make_identity(nc, identity[:])
            nc.vector.memset(ones[:], 1.0)
            table_warmer = held.tile([P, 1], F32, name="table_warmer")
            nc.scalar.activation(table_warmer[:], ones[:, 0:1], ACT.Abs_reciprocal_sqrt)

            for c in range(CHUNKS):
                flipped = banks.tile([D, CHUNK_ROWS], BF16, name=f"flipped{c}", tag="bank")
                for k in range(CHUNK_BLOCKS):
                    nc.tensor.transpose(flipped[:, k * P : (k + 1) * P], rows[c][:, k, :], identity[:])
                window_part = window[:, c * CHUNK_ROWS : (c + 1) * CHUNK_ROWS]
                if c % 2 == 0:
                    nc.vector.tensor_copy(window_part, flipped[:])
                else:
                    nc.scalar.copy(window_part, flipped[:])
            keep_tensor_engine_busy(nc, warm_bank, window[:, 0:WARM_COLS], WARM_COPY)

            hidden = []
            for c in range(PIECES):
                cols, first = PIECE_COLS[c], PIECE_START[c]
                hidden_c = []
                for mb in range(MB):
                    hidden_ps = banks.tile([P, cols], F32, name=f"hidden_ps{c}{mb}", tag="bank")
                    nc.tensor.matmul(
                        hidden_ps[:],
                        w1_sb[:, mb * P : (mb + 1) * P],
                        window[:].indirect(offsets[:, first // 16 : (first + cols) // 16]),
                        start=True,
                        stop=True,
                    )
                    hidden_mb = held.tile([P, cols], BF16, name=f"hidden{c}{mb}")
                    if mb == 0:
                        nc.scalar.activation(hidden_mb[:], hidden_ps[:], ACT.Relu, bias=b1_sb[:, mb : mb + 1])
                    else:
                        nc.vector.tensor_scalar(
                            hidden_mb[:], hidden_ps[:], b1_sb[:, mb : mb + 1], 0.0, op0=ALU.add, op1=ALU.max
                        )
                    hidden_c.append(hidden_mb)
                hidden.append(hidden_c)

            squares = []
            y_ps = []
            sumsq_ps = []
            for c in range(PIECES):
                cols = PIECE_COLS[c]
                block0_and_sum = banks.tile([P, 2, cols], F32, name=f"block0_and_sum{c}", tag="bank")
                block1 = banks.tile([P, cols], F32, name=f"block1{c}", tag="bank")
                y_ps.append([block0_and_sum[:, 0, :], block1[:]])
                sumsq_ps.append(block0_and_sum[:, 1, :])
                squares_c = []
                for qb in range(QB):
                    for mb in range(MB):
                        nc.tensor.matmul(
                            y_ps[c][qb],
                            w2_sb[:, mb, qb * P : (qb + 1) * P],
                            hidden[c][mb][:],
                            start=(mb == 0),
                            stop=(mb == MB - 1),
                        )
                    square_qb = held.tile([P, cols], F32, name=f"square{c}{qb}")
                    nc.scalar.activation(square_qb[:], y_ps[c][qb], ACT.Square, bias=b2_sb[:, qb : qb + 1])
                    squares_c.append(square_qb)
                if c in (0, PIECES - 1):
                    squares.append(squares_c)
                else:
                    both_blocks = held.tile([P, cols], F32, name=f"both_blocks{c}")
                    nc.vector.tensor_tensor(both_blocks[:], squares_c[0][:], squares_c[1][:], ALU.add)
                    squares.append([both_blocks])

            for c in range(PIECES):
                cols, first = PIECE_COLS[c], PIECE_START[c]
                addends = squares[c]
                for i in range(len(addends)):
                    nc.tensor.matmul(
                        sumsq_ps[c], ones[:], addends[i][:], start=(i == 0), stop=(i == len(addends) - 1)
                    )
                inv_norm = held.tile([P, cols], F32, name=f"inv_norm{c}")
                nc.scalar.activation(inv_norm[:], sumsq_ps[c], ACT.Abs_reciprocal_sqrt)
                result = held.tile([P, QB, cols], F32, name=f"result{c}")
                for qb in range(QB):
                    nc.vector.scalar_tensor_tensor(
                        result[:, qb, :], y_ps[c][qb], b2_sb[:, qb : qb + 1], inv_norm[:], op0=ALU.add, op1=ALU.mult
                    )
                    if c == PIECES - 1:
                        nc.sync.dma_start(out_blocked[:, qb, first : first + cols], result[:, qb, :])
                if c < PIECES - 1:
                    nc.sync.dma_start(out_blocked[:, :, first : first + cols], result[:])
